import numpy as np
import ml_dtypes


def mxq(x, axis, fmt="e4m3"):
    dtype, down = {"e4m3": (ml_dtypes.float8_e4m3fn, 7), "e5m2": (ml_dtypes.float8_e5m2, 14)}[fmt]
    v = np.moveaxis(np.asarray(x, np.float32).astype(ml_dtypes.bfloat16).astype(np.float64), axis, -1)
    blocks = v.reshape(v.shape[:-1] + (-1, 32))
    amax = np.abs(blocks).max(-1, keepdims=True)
    byte = np.maximum(np.where(amax > 0, np.frexp(amax)[1] - 1 + 127, 0) - down, 1)
    scale = np.exp2(byte - 127.0)
    codes = (blocks / scale).astype(np.float32).astype(dtype).astype(np.float64)
    return np.moveaxis((codes * scale).reshape(v.shape), -1, axis)


WIDE = False


def mx_kscale(k):
    if not WIDE:
        return np.ones(k)
    levels = np.array([10, -10, 5, -5, 0])
    if k % 512:
        return np.exp2(np.random.permutation(np.resize(levels, k // 32))).repeat(32)
    a = np.empty((k // 512, 16))
    for p in range(k // 512):
        a[p, :8] = np.random.permutation(np.resize(levels, 8))
        for g in range(8):
            far = levels[np.abs(levels - a[p, g]) >= 10]
            a[p, g + 8] = far[np.random.randint(len(far))]
    return np.exp2(a.ravel()).repeat(32)


BF16 = ml_dtypes.bfloat16


def bf(x):
    return np.asarray(x, np.float32).astype(BF16)


def f64(x):
    return np.asarray(x).astype(np.float64)


B, S, D, H, DH, DL, DR = 2, 1024, 8192, 16, 128, 2048, 64
ROPE_BASE = 10000.0


def rope_cos_sin():
    inv_freq = 1.0 / ROPE_BASE ** (np.arange(0, DR, 2) / DR)
    freqs = np.arange(S)[:, None] * inv_freq[None, :]
    emb = np.concatenate([freqs, freqs], axis=-1)
    return np.cos(emb)[None, :, None, :], np.sin(emb)[None, :, None, :]


def rotate_half(u):
    u1, u2 = np.split(u, 2, axis=-1)
    return np.concatenate([-u2, u1], axis=-1)


def setup_inputs():
    s, t = mx_kscale(D), mx_kscale(DL)
    return {"x": bf(np.random.standard_normal((B, S, D)) * s),
            "W_kv_down": bf(np.random.standard_normal((D, DL)) / np.sqrt(D) / s[:, None] * t),
            "W_kv_up": bf(np.random.standard_normal((DL, H * (DH + DR + DH))) / np.sqrt(DL) / t[:, None])}


def reference(x, W_kv_down, W_kv_up):
    kv_latent = mxq(f64(x), 2, "e4m3") @ mxq(f64(W_kv_down), 0, "e4m3")
    kv_full = (mxq(kv_latent, 2, "e4m3") @ mxq(f64(W_kv_up), 0, "e4m3")).reshape(B, S, H, DH + DR + DH)
    k_content = kv_full[..., :DH]
    k_rope = kv_full[..., DH:DH + DR]
    v = kv_full[..., DH + DR:]
    cos, sin = rope_cos_sin()
    k_rope = k_rope * cos + rotate_half(k_rope) * sin
    k = np.concatenate([k_content, k_rope], axis=-1)
    return k, v

@@ -1,0 +1,522 @@
+import math
+from contextlib import ExitStack
+
+import concourse.mybir as mybir
+from concourse.masks import make_identity
+
+FLOPS = 2 * 2048 * 8192 * 2048 + 2 * 2048 * 2048 * 5120
+
+F32 = mybir.dt.float32
+BF16 = mybir.dt.bfloat16
+I32 = mybir.dt.int32
+U32 = mybir.dt.uint32
+U8 = mybir.dt.uint8
+FP8X4 = mybir.dt.float8_e4m3fn_x4
+ALU = mybir.AluOpType
+ACT = mybir.ActivationFunctionType
+
+P = 128
+KIB = 1024
+
+
+def kib(v):
+    return int(round(v * KIB))
+
+
+def tile_multilatentattention_pa_l_kernel(tc, x, w_down, w_up, out_k, out_v):
+    nc = tc.nc
+    xf = x.flatten_outer_dims()
+
+    with ExitStack() as ctx:
+        sb = ctx.enter_context(tc.tile_pool(name="sb", bufs=1))
+        ps = ctx.enter_context(tc.psum_pool(name="ps", bufs=1))
+
+        def slot(shape, dtype, tag, off_kib):
+            return sb.tile(shape, dtype, name=tag, tag=tag, offset=kib(off_kib), align_bytes=256)
+
+        def bank(b):
+            return ps.tile([P, 512], F32, name="bk%d" % b, tag="bk%d" % b)
+
+        state = {"grp": 0, "il": 0, "ql": 0}
+
+        def grp_alloc():
+            k = state["grp"] % 3
+            state["grp"] += 1
+            return slot([P, 2048], BF16, "grp%d" % k, 195.5 + 4 * k)
+
+        def plane_rows(plane, r, c0, c1):
+            return plane[4 * r : P, c0:c1]
+
+        def quantize(codes_ap, plane_ap, in_ap):
+            nc.vector.quantize_mx(out=codes_ap.bitcast(FP8X4), scales=plane_ap, in_=in_ap)
+
+        ident = slot([P, P], F32, "ident", 231.5)
+        make_identity(nc, ident[:])
+        pos = slot([P, 8], F32, "pos", 235)
+        nc.gpsimd.iota(pos[:], pattern=[[P, 8]], base=0, channel_multiplier=1,
+                       allow_small_or_imprecise_dtypes=True)
+        tab = slot([P, 3, 8, 32], F32, "tab", 232)
+
+        ctx.enter_context(tc.manual_schedule())
+
+        warm = slot([P, 1], F32, "warm", 235.25)
+        nc.scalar.activation(out=warm[:], in_=pos[:, 0:1], func=ACT.Sin, scale=0.0)
+
+        xc = {}
+        xp = {}
+        w0c = {}
+        w0p = {}
+        lat = {}
+        latp = {}
+        xraw = {}
+        tps = {}
+        xgs = {}
+        w0raw = {}
+        wgs = {}
+
+        def xload(d):
+            n, gg = divmod(d, 8)
+            t = slot([P, 4, 1024], BF16, "xr%d" % (d % 3), 207.5 + 8 * (d % 3))
+            nc.sync.dma_start(
+                out=t[:],
+                in_=xf[512 * n : 512 * (n + 1), 1024 * gg : 1024 * (gg + 1)].rearrange("(i p) k -> p i k", p=P),
+            )
+            xraw[d] = t
+
+        def transposes(d):
+            words = xraw[d][:].bitcast(F32)
+            for gp in range(2):
+                for ip in range(2):
+                    tp = bank(4 + 2 * gp + ip)
+                    tpv = tp[:].rearrange("p (i u r) -> p i u r", i=2, u=2)
+                    for i2 in range(2):
+                        for u in range(2):
+                            nc.tensor.transpose(
+                                out=tpv[:, i2, u, :],
+                                in_=words[:, 2 * ip + i2, 256 * gp + u : 256 * (gp + 1) : 2],
+                                identity=ident[:],
+                            )
+                    tps[(d, gp, ip)] = tp
+
+        def copy_x(d, gp):
+            xg = grp_alloc()
+            xgw = xg[:].bitcast(F32).rearrange("p (i r u) -> p i r u", i=4, u=2)
+            for ip in range(2):
+                src = tps[(d, gp, ip)][:].rearrange("p (i u r) -> p i r u", i=2, u=2)
+                nc.scalar.copy(out=xgw[:, 2 * ip : 2 * ip + 2, :, :], in_=src)
+            xgs[(d, gp)] = xg
+
+        def quant_x(d, gp):
+            n, gg = divmod(d, 8)
+            g = 2 * gg + gp
+            G, r = divmod(g, 4)
+            xc[(g, n)] = slot([P, 512], U32, "xc%d_%d" % (g, n), 8 * g + 2 * n)
+            if r == 0:
+                xp[(G, n)] = slot([P, 512], U8, "xp%d_%d" % (G, n), 128 + 2 * G + 0.5 * n)
+            quantize(xc[(g, n)][:], plane_rows(xp[(G, n)], r, 0, 512), xgs[(d, gp)][:])
+
+        def wload0(g):
+            k = g % 4
+            t = slot([P, 4, 512], BF16, "w0r%d" % k, 8 * (12 + k) + 4)
+            nc.sync.dma_start(
+                out=t[:], in_=w_down[512 * g : 512 * (g + 1), 0:512].rearrange("(p j) w -> p j w", j=4)
+            )
+            w0raw[g] = t
+
+        def perm_w0(g):
+            wg = grp_alloc()
+            dst = wg[:].rearrange("p (t m j) -> p t m j", t=4, j=4)
+            src = w0raw[g][:].rearrange("p j (m t) -> p t m j", t=4)
+            nc.vector.tensor_copy(out=dst[:, 0:2], in_=src[:, 0:2])
+            if g % 2 == 1:
+                nc.vector.tensor_copy(out=dst[:, 2], in_=src[:, 2])
+                nc.scalar.copy(out=dst[:, 3], in_=src[:, 3])
+            else:
+                nc.scalar.copy(out=dst[:, 2:4], in_=src[:, 2:4])
+            wgs[g] = wg
+
+        def quant_w0(g):
+            G, r = divmod(g, 4)
+            w0c[g] = slot([P, 512], U32, "w0c%d" % g, 136 + 2 * g)
+            if r == 0:
+                w0p[G] = slot([P, 512], U8, "w0p%d" % G, 168 + 0.5 * G)
+            quantize(w0c[g][:], plane_rows(w0p[G], r, 0, 512), wgs[g][:])
+
+        acc = {}
+
+        def matmuls0(d):
+            n, gg = divmod(d, 8)
+            for gp in range(2):
+                g = 2 * gg + gp
+                G, r = divmod(g, 4)
+                for t in range(4):
+                    if g == 0:
+                        acc[t] = bank(t)
+                    nc.tensor.matmul_mx(
+                        out=acc[t][:],
+                        lhsT=w0c[g][:, P * t : P * (t + 1)].bitcast(FP8X4),
+                        lhsT_scale=plane_rows(w0p[G], r, P * t, P * (t + 1)),
+                        rhs=xc[(g, n)][:].bitcast(FP8X4),
+                        rhs_scale=plane_rows(xp[(G, n)], r, 0, 512),
+                        start=(g == 0),
+                        stop=(g == 15),
+                    )
+
+        L_OFF = (187.5, 191.5, 152, 156)
+        il_queue = []
+        ql_queue = []
+
+        def new_l(k):
+            return slot([P, 4, 512], BF16, "L%d" % k, L_OFF[k])
+
+        def evac(engine_is_scalar, dst, src):
+            if engine_is_scalar:
+                nc.scalar.copy(out=dst, in_=src)
+            else:
+                nc.vector.tensor_copy(out=dst, in_=src)
+
+        def interleave_latent(c, n, ltile):
+            lg = grp_alloc()
+            nc.vector.tensor_copy(
+                out=lg[:].rearrange("p (r t) -> p r t", t=4), in_=ltile[:].rearrange("p t r -> p r t")
+            )
+            ql_queue.append((c, n, lg))
+
+        def quant_latent(c, n, lg):
+            if c == 0:
+                lat[(c, n)] = slot([P, 512], U32, "lat0_%d" % n, 170 + 2 * n)
+                latp[n] = slot([P, 512], U8, "latp%d" % n, 178 + 0.5 * n)
+            elif c < 3:
+                lat[(c, n)] = slot([P, 512], U32, "lat%d_%d" % (c, n), 136 + 8 * (c - 1) + 2 * n)
+            else:
+                lat[(c, n)] = slot([P, 512], U32, "lat3_%d" % n, 105 + 2 * n)
+                latp[(3, n)] = slot([P, 512], U8, "latq%d" % n, 113 + 0.5 * n)
+            plane = plane_rows(latp[n], c, 0, 512) if c < 3 else latp[(3, n)][:, :]
+            quantize(lat[(c, n)][:], plane, lg[:])
+
+        def latent_tick():
+            if state["ql"] < len(ql_queue):
+                c, n, lg = ql_queue[state["ql"]]
+                state["ql"] += 1
+                quant_latent(c, n, lg)
+            if state["il"] < len(il_queue):
+                c, n, ltile = il_queue[state["il"]]
+                state["il"] += 1
+                interleave_latent(c, n, ltile)
+
+        tbl = {}
+
+        def table_step(k):
+            if k == 0:
+                tbl["tur"] = slot([P, 2, 8, 32], F32, "tur", 8 * 8 + 4)
+                tbl["nint"] = slot([P, 512], I32, "nint", 8 * 8 + 6)
+                tbl["nflt"] = slot([P, 512], F32, "nflt", 8 * 9 + 4)
+            tur = tbl["tur"]
+            nint = tbl["nint"]
+            nflt = tbl["nflt"]
+            turf = tur[:].rearrange("p s a f -> p (s a f)")
+            if k < 2:
+                for f in range(16 * k, 16 * k + 16):
+                    turns_per_position = 1.0 / (10000.0 ** (f / 32.0)) / (2.0 * math.pi)
+                    nc.vector.tensor_scalar(out=tur[:, 1, :, f], in0=pos[:], scalar1=turns_per_position,
+                                            scalar2=None, op0=ALU.mult)
+            elif k == 2:
+                nc.vector.tensor_scalar(out=tur[:, 0], in0=tur[:, 1], scalar1=0.25, scalar2=None, op0=ALU.add)
+                nc.vector.tensor_copy(out=nint[:], in_=turf)
+            elif k == 3:
+                nc.vector.tensor_copy(out=nflt[:], in_=nint[:])
+                nc.vector.tensor_tensor(out=turf, in0=turf, in1=nflt[:], op=ALU.subtract)
+            elif k == 4:
+                nc.vector.tensor_scalar(out=nflt[:], in0=turf, scalar1=0.5, scalar2=None, op0=ALU.is_gt)
+                nc.vector.tensor_tensor(out=turf, in0=turf, in1=nflt[:], op=ALU.subtract)
+            elif k == 5:
+                nc.vector.tensor_scalar(out=nflt[:], in0=turf, scalar1=-0.5, scalar2=None, op0=ALU.is_lt)
+                nc.vector.tensor_tensor(out=turf, in0=turf, in1=nflt[:], op=ALU.add)
+            elif k == 6:
+                nc.scalar.activation(out=tab[:, 0], in_=tur[:, 0], func=ACT.Sin, scale=2.0 * math.pi)
+                nc.scalar.activation(out=tab[:, 2], in_=tur[:, 1], func=ACT.Sin, scale=2.0 * math.pi)
+                nc.scalar.activation(out=tab[:, 1], in_=tur[:, 1], func=ACT.Sin, scale=-2.0 * math.pi)
+
+        wraw = {}
+        whg = {}
+        wsc = {}
+        wsp = {}
+
+        def split_s(s):
+            return 1 + s // 32, (s // 16) % 2, s % 16
+
+        def wload(s):
+            c, hh, g = split_s(s)
+            k = (s + 4) % 6
+            t = slot([P, 4, 512], BF16, "wr%d" % k, 207.5 + 4 * k)
+            nc.sync.dma_start(
+                out=t[:],
+                in_=w_down[512 * g : 512 * (g + 1), 512 * c : 512 * (c + 1)].rearrange("(p j) w -> p j w", j=4),
+            )
+            wraw[s] = t
+
+        def perm_wh(s):
+            c, hh, g = split_s(s)
+            wg = grp_alloc()
+            dst = wg[:, 0:1024].rearrange("p (t m j) -> p t m j", t=2, j=4)
+            src = wraw[s][:].rearrange("p j (m t) -> p t m j", t=4)
+            nc.scalar.copy(out=dst, in_=src[:, 2 * hh : 2 * hh + 2])
+            whg[s] = wg
+
+        def quant_wh(s):
+            k = s % 6
+            wsc[s] = slot([P, 256], U32, "wsc%d" % k, 180 + k)
+            wsp[s] = slot([P, 256], U8, "wsp%d" % k, 186 + 0.25 * k)
+            quantize(wsc[s][:], wsp[s][:, :], whg[s][:, 0:1024])
+
+        acc1 = {}
+
+        def matmuls1(s):
+            c, hh, g = split_s(s)
+            G, r = divmod(g, 4)
+            for n in range(4):
+                for tt in range(2):
+                    if g == 0:
+                        acc1[(n, tt)] = bank((2 * n + tt + 4) % 8)
+                    nc.tensor.matmul_mx(
+                        out=acc1[(n, tt)][:],
+                        lhsT=wsc[s][:, P * tt : P * (tt + 1)].bitcast(FP8X4),
+                        lhsT_scale=wsp[s][:, P * tt : P * (tt + 1)],
+                        rhs=xc[(g, n)][:].bitcast(FP8X4),
+                        rhs_scale=plane_rows(xp[(G, n)], r, 0, 512),
+                        start=(g == 0),
+                        stop=(g == 15),
+                    )
+
+        SEGS = ((0, 128, 0), (192, 128, 512), (128, 64, 1024))
+        RAWU_OFF = (160, 0, 10)
+        rawu = {}
+        cu = {}
+        pu = {}
+        ugrp = {}
+
+        def loadu(idx):
+            u, g2 = divmod(idx, 4)
+            k = idx % 3
+            t = slot([P, 4, 1280], BF16, "ru%d" % k, RAWU_OFF[k])
+            nc.sync.dma_start(
+                out=t[:],
+                in_=w_up[512 * g2 : 512 * (g2 + 1), 1280 * u : 1280 * (u + 1)].rearrange("(p j) w -> p j w", j=4),
+            )
+            rawu[idx] = t
+
+        def copy_item(item, on_scalar):
+            idx, seg = divmod(item, 3)
+            f0, nf, c0 = SEGS[seg]
+            ug = grp_alloc()
+            dst = ug[:, 0 : 16 * nf].rearrange("p (h c j) -> p h c j", h=4, j=4)
+            src = rawu[idx][:].rearrange("p j (h e) -> p h e j", h=4)[:, :, f0 : f0 + nf, :]
+            evac(on_scalar, dst, src)
+            ugrp[item] = ug
+            if seg == 2 and idx + 3 < 16:
+                loadu(idx + 3)
+
+        def quant_item(item):
+            idx, seg = divmod(item, 3)
+            u, g2 = divmod(idx, 4)
+            f0, nf, c0 = SEGS[seg]
+            if seg == 0:
+                cu[idx] = slot([P, 1280], U32, "cu%d" % idx, 25 + 5 * idx)
+                if g2 == 0:
+                    pu[u] = slot([P, 1280], U8, "pu%d" % u, 20 + 1.25 * u)
+            quantize(cu[idx][:, c0 : c0 + 4 * nf], plane_rows(pu[u], g2, c0, c0 + 4 * nf), ugrp[item][:, 0 : 16 * nf])
+
+        xload(0)
+        wload0(0)
+        wload0(1)
+        xload(1)
+        wload0(2)
+        wload0(3)
+        xload(2)
+
+        def prepare(d):
+            with_w = d < 8
+            copy_x(d, 0)
+            copy_x(d, 1)
+            if with_w:
+                perm_w0(2 * d)
+            quant_x(d, 0)
+            if with_w:
+                perm_w0(2 * d + 1)
+            quant_x(d, 1)
+            if with_w:
+                quant_w0(2 * d)
+                quant_w0(2 * d + 1)
+                if 2 * d + 5 < 16:
+                    wload0(2 * d + 4)
+                    wload0(2 * d + 5)
+
+        for d in range(2):
+            transposes(d)
+            xload(d + 3)
+            prepare(d)
+
+        for d in range(32):
+            n, gg = divmod(d, 8)
+            if d + 2 < 32:
+                transposes(d + 2)
+                if d + 5 < 32:
+                    xload(d + 5)
+            if 27 <= d <= 29:
+                wload(2 * (d - 27))
+                wload(2 * (d - 27) + 1)
+            matmuls0(d)
+            if d + 2 < 32:
+                prepare(d + 2)
+            if gg == 7:
+                ltile = new_l(n % 2)
+                for t in range(4):
+                    evac(t % 2 == 0, ltile[:, t, :], acc[t][:])
+                il_queue.append((0, n, ltile))
+            latent_tick()
+            if 8 <= d < 15:
+                table_step(d - 8)
+            if d == 29:
+                perm_wh(0)
+                perm_wh(1)
+                wload(6)
+                wload(7)
+            if d == 30:
+                quant_wh(0)
+                quant_wh(1)
+                perm_wh(2)
+                perm_wh(3)
+                wload(8)
+            if d == 31:
+                quant_wh(2)
+
+        lt = {}
+        for s in range(96):
+            c, hh, g = split_s(s)
+            if s + 9 < 96:
+                wload(s + 9)
+            if s + 4 < 96:
+                perm_wh(s + 4)
+            if s + 3 < 96:
+                quant_wh(s + 3)
+            matmuls1(s)
+            if g == 15 and s < 95:
+                for n in range(4):
+                    if hh == 0:
+                        lt[n] = new_l(n)
+                    for tt in range(2):
+                        evac(tt == 0, lt[n][:, 2 * hh + tt, :], acc1[(n, tt)][:])
+                    if hh == 1:
+                        il_queue.append((c, n, lt[n]))
+            latent_tick()
+            if s == 70:
+                loadu(0)
+            if s == 81:
+                loadu(1)
+            if s == 82:
+                loadu(2)
+            if 83 <= s < 95:
+                quant_item(s - 83)
+            if 82 <= s < 94:
+                copy_item(s - 82, (s - 82) % 3 == 2)
+
+        evac(True, lt[0][:, 2, :], acc1[(0, 0)][:])
+        evac(False, lt[0][:, 3, :], acc1[(0, 1)][:])
+
+        def latent_now(n):
+            il_queue.append((3, n, lt[n]))
+            latent_tick()
+            latent_tick()
+
+        latent_now(0)
+        for n in range(1, 4):
+            for tt in range(2):
+                evac(True, lt[n][:, 2 + tt, :], acc1[(n, tt)][:])
+        latent_now(1)
+
+        pt = {}
+
+        def passes(q, k, g2s):
+            u, i = divmod(q, 16)
+            n, ii = divmod(i, 4)
+            f0, nf, c0 = SEGS[k]
+            width = 4 * nf
+            for g2 in g2s:
+                if g2 == 0:
+                    pt[(q, k)] = bank((3 * q + k + 4) % 8)
+                if g2 < 3:
+                    lsc = plane_rows(latp[n], g2, P * ii, P * (ii + 1))
+                else:
+                    lsc = latp[(3, n)][:, P * ii : P * (ii + 1)]
+                nc.tensor.matmul_mx(
+                    out=pt[(q, k)][:, 0:width],
+                    lhsT=lat[(g2, n)][:, P * ii : P * (ii + 1)].bitcast(FP8X4),
+                    lhsT_scale=lsc,
+                    rhs=cu[4 * u + g2][:, c0 : c0 + width].bitcast(FP8X4),
+                    rhs_scale=plane_rows(pu[u], g2, c0, c0 + width),
+                    start=(g2 == 0),
+                    stop=(g2 == 3),
+                )
+
+        def finish(q):
+            u, i = divmod(q, 16)
+            b, a = divmod(i, 8)
+            k3 = q % 3
+            k2 = q % 2
+            ko = slot([P, 4, 192], F32, "ko%d" % k3, 207.5 + 3 * k3)
+            vo = slot([P, 512], F32, "vo%d" % k3, 216.5 + 2 * k3)
+            ta = slot([P, 256], F32, "ta%d" % k2, 222.5 + k2)
+            tb = slot([P, 256], F32, "tb%d" % k2, 224.5 + k2)
+            nc.scalar.copy(out=ko[:, :, 0:128], in_=pt[(q, 0)][:].rearrange("p (h c) -> p h c", h=4))
+            nc.scalar.copy(out=vo[:], in_=pt[(q, 1)][:])
+            rope = pt[(q, 2)][:, 0:256]
+            r4 = rope.rearrange("p (h s f) -> p h s f", h=4, s=2)
+            tb4 = tb[:].rearrange("p (h s f) -> p h s f", h=4, s=2)
+            nc.vector.tensor_tensor(
+                out=ta[:].rearrange("p (e f) -> p e f", f=32),
+                in0=rope.rearrange("p (e f) -> p e f", f=32),
+                in1=tab[:, 0, a, :].unsqueeze(1).to_broadcast([P, 8, 32]),
+                op=ALU.mult,
+            )
+            for half in range(2):
+                nc.vector.tensor_tensor(
+                    out=tb4[:, :, half, :],
+                    in0=r4[:, :, 1 - half, :],
+                    in1=tab[:, 1 + half, a, :].unsqueeze(1).to_broadcast([P, 4, 32]),
+                    op=ALU.mult,
+                )
+            nc.vector.tensor_tensor(
+                out=ko[:, :, 128:192],
+                in0=ta[:].rearrange("p (h e) -> p h e", h=4),
+                in1=tb[:].rearrange("p (h e) -> p h e", h=4),
+                op=ALU.add,
+            )
+            rows = slice(P * a, P * (a + 1))
+            heads = slice(4 * u, 4 * (u + 1))
+            nc.sync.dma_start(out=out_v[b, rows, heads, :], in_=vo[:].rearrange("p (h c) -> p h c", h=4))
+            nc.sync.dma_start(out=out_k[b, rows, heads, :], in_=ko[:])
+
+        items = {"copied": 12, "quantized": 12}
+
+        def produce(q):
+            if items["quantized"] < items["copied"]:
+                quant_item(items["quantized"])
+                items["quantized"] += 1
+            if (q < 12 or q % 4 != 3) and items["copied"] < 48:
+                copy_item(items["copied"], items["copied"] % 3 != 0)
+                items["copied"] += 1
+
+        for q in range(2):
+            for k in range(3):
+                passes(q, k, (0, 1, 2))
+        for q in range(2):
+            for k in range(3):
+                passes(q, k, (3,))
+            finish(q)
+            latent_now(2 + q)
+            produce(q)
+        for q in range(2, 64):
+            for k in range(3):
+                passes(q, k, (0, 1, 2, 3))
+            finish(q)
+            produce(q)

@@ -17,6 +17,7 @@ ACT = mybir.ActivationFunctionType
 
 P = 128
 KIB = 1024
+FIRST_SORTED = 8
 
 
 def kib(v):
@@ -83,6 +84,18 @@ def tile_multilatentattention_pa_l_kernel(tc, x, w_down, w_up, out_k, out_v):
             )
             xraw[d] = t
 
+        XS_OFF = (180, 191.5)
+        xsorted = {}
+
+        def sort_x(d):
+            words = xraw[d][:].bitcast(F32)
+            for gp in range(2):
+                xs = slot([P, 4, 2, P], F32, "xs%d" % gp, XS_OFF[gp])
+                nc.vector.tensor_copy(
+                    out=xs[:], in_=words[:, :, 256 * gp : 256 * (gp + 1)].rearrange("p i (m u) -> p i u m", u=2)
+                )
+                xsorted[(d, gp)] = xs
+
         def transposes(d):
             words = xraw[d][:].bitcast(F32)
             for gp in range(2):
@@ -91,11 +104,11 @@ def tile_multilatentattention_pa_l_kernel(tc, x, w_down, w_up, out_k, out_v):
                     tpv = tp[:].rearrange("p (i u r) -> p i u r", i=2, u=2)
                     for i2 in range(2):
                         for u in range(2):
-                            nc.tensor.transpose(
-                                out=tpv[:, i2, u, :],
-                                in_=words[:, 2 * ip + i2, 256 * gp + u : 256 * (gp + 1) : 2],
-                                identity=ident[:],
-                            )
+                            if d < FIRST_SORTED:
+                                src = words[:, 2 * ip + i2, 256 * gp + u : 256 * (gp + 1) : 2]
+                            else:
+                                src = xsorted[(d, gp)][:, 2 * ip + i2, u, :]
+                            nc.tensor.transpose(out=tpv[:, i2, u, :], in_=src, identity=ident[:])
                     tps[(d, gp, ip)] = tp
 
         def copy_x(d, gp):
@@ -260,7 +273,7 @@ def tile_multilatentattention_pa_l_kernel(tc, x, w_down, w_up, out_k, out_v):
             wg = grp_alloc()
             dst = wg[:, 0:1024].rearrange("p (t m j) -> p t m j", t=2, j=4)
             src = wraw[s][:].rearrange("p j (m t) -> p t m j", t=4)
-            nc.scalar.copy(out=dst, in_=src[:, 2 * hh : 2 * hh + 2])
+            evac(s % 2 == 0 or s >= 80, dst, src[:, 2 * hh : 2 * hh + 2])
             whg[s] = wg
 
         def quant_wh(s):
@@ -360,16 +373,20 @@ def tile_multilatentattention_pa_l_kernel(tc, x, w_down, w_up, out_k, out_v):
             n, gg = divmod(d, 8)
             if d + 2 < 32:
                 transposes(d + 2)
-                if d + 5 < 32:
+                if d + 2 < FIRST_SORTED:
                     xload(d + 5)
             if 27 <= d <= 29:
                 wload(2 * (d - 27))
                 wload(2 * (d - 27) + 1)
             matmuls0(d)
+            if FIRST_SORTED <= d + 3 < 32:
+                sort_x(d + 3)
+                if d + 6 < 32:
+                    xload(d + 6)
             if d + 2 < 32:
                 prepare(d + 2)
             if gg == 7:
-                ltile = new_l(n % 2)
+                ltile = new_l(0)
                 for t in range(4):
                     evac(t % 2 == 0, ltile[:, t, :], acc[t][:])
                 il_queue.append((0, n, ltile))
@@ -435,6 +452,7 @@ def tile_multilatentattention_pa_l_kernel(tc, x, w_down, w_up, out_k, out_v):
         latent_now(1)
 
         pt = {}
+        GROUP_ORDER = (2, 0, 1)
 
         def passes(q, k, g2s):
             u, i = divmod(q, 16)
@@ -443,7 +461,7 @@ def tile_multilatentattention_pa_l_kernel(tc, x, w_down, w_up, out_k, out_v):
             width = 4 * nf
             for g2 in g2s:
                 if g2 == 0:
-                    pt[(q, k)] = bank((3 * q + k + 4) % 8)
+                    pt[(q, k)] = bank((3 * q + GROUP_ORDER.index(k) + 4) % 8)
                 if g2 < 3:
                     lsc = plane_rows(latp[n], g2, P * ii, P * (ii + 1))
                 else:
@@ -461,12 +479,12 @@ def tile_multilatentattention_pa_l_kernel(tc, x, w_down, w_up, out_k, out_v):
         def finish(q):
             u, i = divmod(q, 16)
             b, a = divmod(i, 8)
-            k3 = q % 3
+            k6 = q % 6
             k2 = q % 2
-            ko = slot([P, 4, 192], F32, "ko%d" % k3, 207.5 + 3 * k3)
-            vo = slot([P, 512], F32, "vo%d" % k3, 216.5 + 2 * k3)
-            ta = slot([P, 256], F32, "ta%d" % k2, 222.5 + k2)
-            tb = slot([P, 256], F32, "tb%d" % k2, 224.5 + k2)
+            ko = slot([P, 4, 192], F32, "ko%d" % k6, 207.5 + 3 * k6)
+            vo = slot([P, 512], F32, "vo%d" % k6, 115 + 2 * k6)
+            ta = slot([P, 256], F32, "ta%d" % k2, 225.5 + k2)
+            tb = slot([P, 256], F32, "tb%d" % k2, 227.5 + k2)
             nc.scalar.copy(out=ko[:, :, 0:128], in_=pt[(q, 0)][:].rearrange("p (h c) -> p h c", h=4))
             nc.scalar.copy(out=vo[:], in_=pt[(q, 1)][:])
             rope = pt[(q, 2)][:, 0:256]
@@ -507,16 +525,16 @@ def tile_multilatentattention_pa_l_kernel(tc, x, w_down, w_up, out_k, out_v):
                 items["copied"] += 1
 
         for q in range(2):
-            for k in range(3):
+            for k in GROUP_ORDER:
                 passes(q, k, (0, 1, 2))
         for q in range(2):
-            for k in range(3):
+            for k in GROUP_ORDER:
                 passes(q, k, (3,))
             finish(q)
             latent_now(2 + q)
             produce(q)
         for q in range(2, 64):
-            for k in range(3):
+            for k in GROUP_ORDER:
                 passes(q, k, (0, 1, 2, 3))
             finish(q)
             produce(q)

@@ -18,6 +18,7 @@ ACT = mybir.ActivationFunctionType
 P = 128
 KIB = 1024
 FIRST_SORTED = 8
+STAT_SHIFT = 64
 
 
 def kib(v):
@@ -32,8 +33,9 @@ def tile_multilatentattention_pa_l_kernel(tc, x, w_down, w_up, out_k, out_v):
         sb = ctx.enter_context(tc.tile_pool(name="sb", bufs=1))
         ps = ctx.enter_context(tc.psum_pool(name="ps", bufs=1))
 
-        def slot(shape, dtype, tag, off_kib):
-            return sb.tile(shape, dtype, name=tag, tag=tag, offset=kib(off_kib), align_bytes=256)
+        def slot(shape, dtype, tag, off_kib, shift=0):
+            return sb.tile(shape, dtype, name=tag, tag=tag, offset=kib(off_kib) + shift,
+                           align_bytes=(256 if shift == 0 else 64))
 
         def bank(b):
             return ps.tile([P, 512], F32, name="bk%d" % b, tag="bk%d" % b)
@@ -43,7 +45,7 @@ def tile_multilatentattention_pa_l_kernel(tc, x, w_down, w_up, out_k, out_v):
         def grp_alloc():
             k = state["grp"] % 3
             state["grp"] += 1
-            return slot([P, 2048], BF16, "grp%d" % k, 195.5 + 4 * k)
+            return slot([P, 2048], BF16, "grp%d" % k, 198.25 + 4 * k)
 
         def plane_rows(plane, r, c0, c1):
             return plane[4 * r : P, c0:c1]
@@ -51,16 +53,16 @@ def tile_multilatentattention_pa_l_kernel(tc, x, w_down, w_up, out_k, out_v):
         def quantize(codes_ap, plane_ap, in_ap):
             nc.vector.quantize_mx(out=codes_ap.bitcast(FP8X4), scales=plane_ap, in_=in_ap)
 
-        ident = slot([P, P], F32, "ident", 231.5)
+        ident = slot([P, P], F32, "ident", 234.25)
         make_identity(nc, ident[:])
-        pos = slot([P, 8], F32, "pos", 235)
+        pos = slot([P, 8], F32, "pos", 237.75)
         nc.gpsimd.iota(pos[:], pattern=[[P, 8]], base=0, channel_multiplier=1,
                        allow_small_or_imprecise_dtypes=True)
-        tab = slot([P, 3, 8, 32], F32, "tab", 232)
+        tab = slot([P, 3, 8, 32], F32, "tab", 234.75)
 
         ctx.enter_context(tc.manual_schedule())
 
-        warm = slot([P, 1], F32, "warm", 235.25)
+        warm = slot([P, 1], F32, "warm", 238)
         nc.scalar.activation(out=warm[:], in_=pos[:, 0:1], func=ACT.Sin, scale=0.0)
 
         xc = {}
@@ -77,14 +79,14 @@ def tile_multilatentattention_pa_l_kernel(tc, x, w_down, w_up, out_k, out_v):
 
         def xload(d):
             n, gg = divmod(d, 8)
-            t = slot([P, 4, 1024], BF16, "xr%d" % (d % 3), 207.5 + 8 * (d % 3))
+            t = slot([P, 4, 1024], BF16, "xr%d" % (d % 3), 210.25 + 8 * (d % 3))
             nc.sync.dma_start(
                 out=t[:],
                 in_=xf[512 * n : 512 * (n + 1), 1024 * gg : 1024 * (gg + 1)].rearrange("(i p) k -> p i k", p=P),
             )
             xraw[d] = t
 
-        XS_OFF = (180, 191.5)
+        XS_OFF = (182.5, 194.25)
         xsorted = {}
 
         def sort_x(d):
@@ -149,11 +151,11 @@ def tile_multilatentattention_pa_l_kernel(tc, x, w_down, w_up, out_k, out_v):
             wgs[g] = wg
 
         def quant_w0(g):
-            G, r = divmod(g, 4)
-            w0c[g] = slot([P, 512], U32, "w0c%d" % g, 136 + 2 * g)
-            if r == 0:
-                w0p[G] = slot([P, 512], U8, "w0p%d" % G, 168 + 0.5 * G)
-            quantize(w0c[g][:], plane_rows(w0p[G], r, 0, 512), wgs[g][:])
+            gg, gp = divmod(g, 2)
+            w0c[g] = slot([P, 512], U32, "w0c%d" % g, 136 + 2 * g, STAT_SHIFT)
+            if gp == 0:
+                w0p[gg] = slot([P, 512], U8, "w0p%d" % gg, 168.25 + 0.5 * gg)
+            quantize(w0c[g][:], plane_rows(w0p[gg], gp, 0, 512), wgs[g][:])
 
         acc = {}
 
@@ -168,14 +170,14 @@ def tile_multilatentattention_pa_l_kernel(tc, x, w_down, w_up, out_k, out_v):
                     nc.tensor.matmul_mx(
                         out=acc[t][:],
                         lhsT=w0c[g][:, P * t : P * (t + 1)].bitcast(FP8X4),
-                        lhsT_scale=plane_rows(w0p[G], r, P * t, P * (t + 1)),
+                        lhsT_scale=plane_rows(w0p[gg], gp, P * t, P * (t + 1)),
                         rhs=xc[(g, n)][:].bitcast(FP8X4),
                         rhs_scale=plane_rows(xp[(G, n)], r, 0, 512),
                         start=(g == 0),
                         stop=(g == 15),
                     )
 
-        L_OFF = (187.5, 191.5, 152, 156)
+        L_OFF = (190.25, 194.25, 152.25, 156.25)
         il_queue = []
         ql_queue = []
 
@@ -197,13 +199,13 @@ def tile_multilatentattention_pa_l_kernel(tc, x, w_down, w_up, out_k, out_v):
 
         def quant_latent(c, n, lg):
             if c == 0:
-                lat[(c, n)] = slot([P, 512], U32, "lat0_%d" % n, 170 + 2 * n)
-                latp[n] = slot([P, 512], U8, "latp%d" % n, 178 + 0.5 * n)
+                lat[(c, n)] = slot([P, 512], U32, "lat0_%d" % n, 172.25 + 2 * n, STAT_SHIFT)
+                latp[n] = slot([P, 512], U8, "latp%d" % n, 180.5 + 0.5 * n)
             elif c < 3:
-                lat[(c, n)] = slot([P, 512], U32, "lat%d_%d" % (c, n), 136 + 8 * (c - 1) + 2 * n)
+                lat[(c, n)] = slot([P, 512], U32, "lat%d_%d" % (c, n), 136 + 8 * (c - 1) + 2 * n, STAT_SHIFT)
             else:
-                lat[(c, n)] = slot([P, 512], U32, "lat3_%d" % n, 105 + 2 * n)
-                latp[(3, n)] = slot([P, 512], U8, "latq%d" % n, 113 + 0.5 * n)
+                lat[(c, n)] = slot([P, 512], U32, "lat3_%d" % n, 105 + 2 * n, STAT_SHIFT)
+                latp[(3, n)] = slot([P, 512], U8, "latq%d" % n, 113.25 + 0.5 * n)
             plane = plane_rows(latp[n], c, 0, 512) if c < 3 else latp[(3, n)][:, :]
             quantize(lat[(c, n)][:], plane, lg[:])
 
@@ -261,7 +263,7 @@ def tile_multilatentattention_pa_l_kernel(tc, x, w_down, w_up, out_k, out_v):
         def wload(s):
             c, hh, g = split_s(s)
             k = (s + 4) % 6
-            t = slot([P, 4, 512], BF16, "wr%d" % k, 207.5 + 4 * k)
+            t = slot([P, 4, 512], BF16, "wr%d" % k, 210.25 + 4 * k)
             nc.sync.dma_start(
                 out=t[:],
                 in_=w_down[512 * g : 512 * (g + 1), 512 * c : 512 * (c + 1)].rearrange("(p j) w -> p j w", j=4),
@@ -278,8 +280,8 @@ def tile_multilatentattention_pa_l_kernel(tc, x, w_down, w_up, out_k, out_v):
 
         def quant_wh(s):
             k = s % 6
-            wsc[s] = slot([P, 256], U32, "wsc%d" % k, 180 + k)
-            wsp[s] = slot([P, 256], U8, "wsp%d" % k, 186 + 0.25 * k)
+            wsc[s] = slot([P, 256], U32, "wsc%d" % k, 182.5 + k, STAT_SHIFT)
+            wsp[s] = slot([P, 256], U8, "wsp%d" % k, 188.75 + 0.25 * k)
             quantize(wsc[s][:], wsp[s][:, :], whg[s][:, 0:1024])
 
         acc1 = {}
@@ -302,7 +304,7 @@ def tile_multilatentattention_pa_l_kernel(tc, x, w_down, w_up, out_k, out_v):
                     )
 
         SEGS = ((0, 128, 0), (192, 128, 512), (128, 64, 1024))
-        RAWU_OFF = (160, 0, 10)
+        RAWU_OFF = (160.25, 0, 10)
         rawu = {}
         cu = {}
         pu = {}
@@ -351,13 +353,11 @@ def tile_multilatentattention_pa_l_kernel(tc, x, w_down, w_up, out_k, out_v):
             with_w = d < 8
             copy_x(d, 0)
             copy_x(d, 1)
-            if with_w:
-                perm_w0(2 * d)
             quant_x(d, 0)
-            if with_w:
-                perm_w0(2 * d + 1)
             quant_x(d, 1)
             if with_w:
+                perm_w0(2 * d)
+                perm_w0(2 * d + 1)
                 quant_w0(2 * d)
                 quant_w0(2 * d + 1)
                 if 2 * d + 5 < 16:
@@ -481,10 +481,10 @@ def tile_multilatentattention_pa_l_kernel(tc, x, w_down, w_up, out_k, out_v):
             b, a = divmod(i, 8)
             k6 = q % 6
             k2 = q % 2
-            ko = slot([P, 4, 192], F32, "ko%d" % k6, 207.5 + 3 * k6)
-            vo = slot([P, 512], F32, "vo%d" % k6, 115 + 2 * k6)
-            ta = slot([P, 256], F32, "ta%d" % k2, 225.5 + k2)
-            tb = slot([P, 256], F32, "tb%d" % k2, 227.5 + k2)
+            ko = slot([P, 4, 192], F32, "ko%d" % k6, 210.25 + 3 * k6)
+            vo = slot([P, 512], F32, "vo%d" % k6, 115.25 + 2 * k6)
+            ta = slot([P, 256], F32, "ta%d" % k2, 228.25 + k2)
+            tb = slot([P, 256], F32, "tb%d" % k2, 230.25 + k2)
             nc.scalar.copy(out=ko[:, :, 0:128], in_=pt[(q, 0)][:].rearrange("p (h c) -> p h c", h=4))
             nc.scalar.copy(out=vo[:], in_=pt[(q, 1)][:])
             rope = pt[(q, 2)][:, 0:256]

import math
from contextlib import ExitStack

import concourse.mybir as mybir
from concourse.masks import make_identity

FLOPS = 2 * 2048 * 8192 * 2048 + 2 * 2048 * 2048 * 5120

F32 = mybir.dt.float32
BF16 = mybir.dt.bfloat16
I32 = mybir.dt.int32
U32 = mybir.dt.uint32
U8 = mybir.dt.uint8
FP8X4 = mybir.dt.float8_e4m3fn_x4
ALU = mybir.AluOpType
ACT = mybir.ActivationFunctionType

P = 128
KIB = 1024
FIRST_SORTED = 8
STAT_SHIFT = 64


def kib(v):
    return int(round(v * KIB))


def tile_multilatentattention_pa_l_kernel(tc, x, w_down, w_up, out_k, out_v):
    nc = tc.nc
    xf = x.flatten_outer_dims()

    with ExitStack() as ctx:
        sb = ctx.enter_context(tc.tile_pool(name="sb", bufs=1))
        ps = ctx.enter_context(tc.psum_pool(name="ps", bufs=1))

        def slot(shape, dtype, tag, off_kib, shift=0):
            return sb.tile(shape, dtype, name=tag, tag=tag, offset=kib(off_kib) + shift,
                           align_bytes=(256 if shift == 0 else 64))

        def bank(b):
            return ps.tile([P, 512], F32, name="bk%d" % b, tag="bk%d" % b)

        state = {"grp": 0, "il": 0, "ql": 0}

        def grp_alloc():
            k = state["grp"] % 3
            state["grp"] += 1
            return slot([P, 2048], BF16, "grp%d" % k, 198.25 + 4 * k)

        def plane_rows(plane, r, c0, c1):
            return plane[4 * r : P, c0:c1]

        def quantize(codes_ap, plane_ap, in_ap):
            nc.vector.quantize_mx(out=codes_ap.bitcast(FP8X4), scales=plane_ap, in_=in_ap)

        ident = slot([P, P], F32, "ident", 234.25)
        make_identity(nc, ident[:])
        pos = slot([P, 8], F32, "pos", 237.75)
        nc.gpsimd.iota(pos[:], pattern=[[P, 8]], base=0, channel_multiplier=1,
                       allow_small_or_imprecise_dtypes=True)
        tab = slot([P, 3, 8, 32], F32, "tab", 234.75)

        ctx.enter_context(tc.manual_schedule())

        warm = slot([P, 1], F32, "warm", 238)
        nc.scalar.activation(out=warm[:], in_=pos[:, 0:1], func=ACT.Sin, scale=0.0)

        xc = {}
        xp = {}
        w0c = {}
        w0p = {}
        lat = {}
        latp = {}
        xraw = {}
        tps = {}
        xgs = {}
        w0raw = {}
        wgs = {}

        def xload(d):
            n, gg = divmod(d, 8)
            t = slot([P, 4, 1024], BF16, "xr%d" % (d % 3), 210.25 + 8 * (d % 3))
            nc.sync.dma_start(
                out=t[:],
                in_=xf[512 * n : 512 * (n + 1), 1024 * gg : 1024 * (gg + 1)].rearrange("(i p) k -> p i k", p=P),
            )
            xraw[d] = t

        XS_OFF = (182.5, 194.25)
        xsorted = {}

        def sort_x(d):
            words = xraw[d][:].bitcast(F32)
            for gp in range(2):
                xs = slot([P, 4, 2, P], F32, "xs%d" % gp, XS_OFF[gp])
                nc.vector.tensor_copy(
                    out=xs[:], in_=words[:, :, 256 * gp : 256 * (gp + 1)].rearrange("p i (m u) -> p i u m", u=2)
                )
                xsorted[(d, gp)] = xs

        def transposes(d):
            words = xraw[d][:].bitcast(F32)
            for gp in range(2):
                for ip in range(2):
                    tp = bank(4 + 2 * gp + ip)
                    tpv = tp[:].rearrange("p (i u r) -> p i u r", i=2, u=2)
                    for i2 in range(2):
                        for u in range(2):
                            if d < FIRST_SORTED:
                                src = words[:, 2 * ip + i2, 256 * gp + u : 256 * (gp + 1) : 2]
                            else:
                                src = xsorted[(d, gp)][:, 2 * ip + i2, u, :]
                            nc.tensor.transpose(out=tpv[:, i2, u, :], in_=src, identity=ident[:])
                    tps[(d, gp, ip)] = tp

        def copy_x(d, gp):
            xg = grp_alloc()
            xgw = xg[:].bitcast(F32).rearrange("p (i r u) -> p i r u", i=4, u=2)
            for ip in range(2):
                src = tps[(d, gp, ip)][:].rearrange("p (i u r) -> p i r u", i=2, u=2)
                nc.scalar.copy(out=xgw[:, 2 * ip : 2 * ip + 2, :, :], in_=src)
            xgs[(d, gp)] = xg

        def quant_x(d, gp):
            n, gg = divmod(d, 8)
            g = 2 * gg + gp
            G, r = divmod(g, 4)
            xc[(g, n)] = slot([P, 512], U32, "xc%d_%d" % (g, n), 8 * g + 2 * n)
            if r == 0:
                xp[(G, n)] = slot([P, 512], U8, "xp%d_%d" % (G, n), 128 + 2 * G + 0.5 * n)
            quantize(xc[(g, n)][:], plane_rows(xp[(G, n)], r, 0, 512), xgs[(d, gp)][:])

        def wload0(g):
            k = g % 4
            t = slot([P, 4, 512], BF16, "w0r%d" % k, 8 * (12 + k) + 4)
            nc.sync.dma_start(
                out=t[:], in_=w_down[512 * g : 512 * (g + 1), 0:512].rearrange("(p j) w -> p j w", j=4)
            )
            w0raw[g] = t

        def perm_w0(g):
            wg = grp_alloc()
            dst = wg[:].rearrange("p (t m j) -> p t m j", t=4, j=4)
            src = w0raw[g][:].rearrange("p j (m t) -> p t m j", t=4)
            nc.vector.tensor_copy(out=dst[:, 0:2], in_=src[:, 0:2])
            if g % 2 == 1:
                nc.vector.tensor_copy(out=dst[:, 2], in_=src[:, 2])
                nc.scalar.copy(out=dst[:, 3], in_=src[:, 3])
            else:
                nc.scalar.copy(out=dst[:, 2:4], in_=src[:, 2:4])
            wgs[g] = wg

        def quant_w0(g):
            gg, gp = divmod(g, 2)
            w0c[g] = slot([P, 512], U32, "w0c%d" % g, 136 + 2 * g, STAT_SHIFT)
            if gp == 0:
                w0p[gg] = slot([P, 512], U8, "w0p%d" % gg, 168.25 + 0.5 * gg)
            quantize(w0c[g][:], plane_rows(w0p[gg], gp, 0, 512), wgs[g][:])

        acc = {}

        def matmuls0(d):
            n, gg = divmod(d, 8)
            for gp in range(2):
                g = 2 * gg + gp
                G, r = divmod(g, 4)
                for t in range(4):
                    if g == 0:
                        acc[t] = bank(t)
                    nc.tensor.matmul_mx(
                        out=acc[t][:],
                        lhsT=w0c[g][:, P * t : P * (t + 1)].bitcast(FP8X4),
                        lhsT_scale=plane_rows(w0p[gg], gp, P * t, P * (t + 1)),
                        rhs=xc[(g, n)][:].bitcast(FP8X4),
                        rhs_scale=plane_rows(xp[(G, n)], r, 0, 512),
                        start=(g == 0),
                        stop=(g == 15),
                    )

        L_OFF = (190.25, 194.25, 152.25, 156.25)
        il_queue = []
        ql_queue = []

        def new_l(k):
            return slot([P, 4, 512], BF16, "L%d" % k, L_OFF[k])

        def evac(engine_is_scalar, dst, src):
            if engine_is_scalar:
                nc.scalar.copy(out=dst, in_=src)
            else:
                nc.vector.tensor_copy(out=dst, in_=src)

        def interleave_latent(c, n, ltile):
            lg = grp_alloc()
            nc.vector.tensor_copy(
                out=lg[:].rearrange("p (r t) -> p r t", t=4), in_=ltile[:].rearrange("p t r -> p r t")
            )
            ql_queue.append((c, n, lg))

        def quant_latent(c, n, lg):
            if c == 0:
                lat[(c, n)] = slot([P, 512], U32, "lat0_%d" % n, 172.25 + 2 * n, STAT_SHIFT)
                latp[n] = slot([P, 512], U8, "latp%d" % n, 180.5 + 0.5 * n)
            elif c < 3:
                lat[(c, n)] = slot([P, 512], U32, "lat%d_%d" % (c, n), 136 + 8 * (c - 1) + 2 * n, STAT_SHIFT)
            else:
                lat[(c, n)] = slot([P, 512], U32, "lat3_%d" % n, 105 + 2 * n, STAT_SHIFT)
                latp[(3, n)] = slot([P, 512], U8, "latq%d" % n, 113.25 + 0.5 * n)
            plane = plane_rows(latp[n], c, 0, 512) if c < 3 else latp[(3, n)][:, :]
            quantize(lat[(c, n)][:], plane, lg[:])

        def latent_tick():
            if state["ql"] < len(ql_queue):
                c, n, lg = ql_queue[state["ql"]]
                state["ql"] += 1
                quant_latent(c, n, lg)
            if state["il"] < len(il_queue):
                c, n, ltile = il_queue[state["il"]]
                state["il"] += 1
                interleave_latent(c, n, ltile)

        tbl = {}

        def table_step(k):
            if k == 0:
                tbl["tur"] = slot([P, 2, 8, 32], F32, "tur", 8 * 8 + 4)
                tbl["nint"] = slot([P, 512], I32, "nint", 8 * 8 + 6)
                tbl["nflt"] = slot([P, 512], F32, "nflt", 8 * 9 + 4)
            tur = tbl["tur"]
            nint = tbl["nint"]
            nflt = tbl["nflt"]
            turf = tur[:].rearrange("p s a f -> p (s a f)")
            if k < 2:
                for f in range(16 * k, 16 * k + 16):
                    turns_per_position = 1.0 / (10000.0 ** (f / 32.0)) / (2.0 * math.pi)
                    nc.vector.tensor_scalar(out=tur[:, 1, :, f], in0=pos[:], scalar1=turns_per_position,
                                            scalar2=None, op0=ALU.mult)
            elif k == 2:
                nc.vector.tensor_scalar(out=tur[:, 0], in0=tur[:, 1], scalar1=0.25, scalar2=None, op0=ALU.add)
                nc.vector.tensor_copy(out=nint[:], in_=turf)
            elif k == 3:
                nc.vector.tensor_copy(out=nflt[:], in_=nint[:])
                nc.vector.tensor_tensor(out=turf, in0=turf, in1=nflt[:], op=ALU.subtract)
            elif k == 4:
                nc.vector.tensor_scalar(out=nflt[:], in0=turf, scalar1=0.5, scalar2=None, op0=ALU.is_gt)
                nc.vector.tensor_tensor(out=turf, in0=turf, in1=nflt[:], op=ALU.subtract)
            elif k == 5:
                nc.vector.tensor_scalar(out=nflt[:], in0=turf, scalar1=-0.5, scalar2=None, op0=ALU.is_lt)
                nc.vector.tensor_tensor(out=turf, in0=turf, in1=nflt[:], op=ALU.add)
            elif k == 6:
                nc.scalar.activation(out=tab[:, 0], in_=tur[:, 0], func=ACT.Sin, scale=2.0 * math.pi)
                nc.scalar.activation(out=tab[:, 2], in_=tur[:, 1], func=ACT.Sin, scale=2.0 * math.pi)
                nc.scalar.activation(out=tab[:, 1], in_=tur[:, 1], func=ACT.Sin, scale=-2.0 * math.pi)

        wraw = {}
        whg = {}
        wsc = {}
        wsp = {}

        def split_s(s):
            return 1 + s // 32, (s // 16) % 2, s % 16

        def wload(s):
            c, hh, g = split_s(s)
            k = (s + 4) % 6
            t = slot([P, 4, 512], BF16, "wr%d" % k, 210.25 + 4 * k)
            nc.sync.dma_start(
                out=t[:],
                in_=w_down[512 * g : 512 * (g + 1), 512 * c : 512 * (c + 1)].rearrange("(p j) w -> p j w", j=4),
            )
            wraw[s] = t

        def perm_wh(s):
            c, hh, g = split_s(s)
            wg = grp_alloc()
            dst = wg[:, 0:1024].rearrange("p (t m j) -> p t m j", t=2, j=4)
            src = wraw[s][:].rearrange("p j (m t) -> p t m j", t=4)
            evac(s % 2 == 0 or s >= 80, dst, src[:, 2 * hh : 2 * hh + 2])
            whg[s] = wg

        def quant_wh(s):
            k = s % 6
            wsc[s] = slot([P, 256], U32, "wsc%d" % k, 182.5 + k, STAT_SHIFT)
            wsp[s] = slot([P, 256], U8, "wsp%d" % k, 188.75 + 0.25 * k)
            quantize(wsc[s][:], wsp[s][:, :], whg[s][:, 0:1024])

        acc1 = {}

        def matmuls1(s):
            c, hh, g = split_s(s)
            G, r = divmod(g, 4)
            for n in range(4):
                for tt in range(2):
                    if g == 0:
                        acc1[(n, tt)] = bank((2 * n + tt + 4) % 8)
                    nc.tensor.matmul_mx(
                        out=acc1[(n, tt)][:],
                        lhsT=wsc[s][:, P * tt : P * (tt + 1)].bitcast(FP8X4),
                        lhsT_scale=wsp[s][:, P * tt : P * (tt + 1)],
                        rhs=xc[(g, n)][:].bitcast(FP8X4),
                        rhs_scale=plane_rows(xp[(G, n)], r, 0, 512),
                        start=(g == 0),
                        stop=(g == 15),
                    )

        SEGS = ((0, 128, 0), (192, 128, 512), (128, 64, 1024))
        RAWU_OFF = (160.25, 0, 10)
        rawu = {}
        cu = {}
        pu = {}
        ugrp = {}

        def loadu(idx):
            u, g2 = divmod(idx, 4)
            k = idx % 3
            t = slot([P, 4, 1280], BF16, "ru%d" % k, RAWU_OFF[k])
            nc.sync.dma_start(
                out=t[:],
                in_=w_up[512 * g2 : 512 * (g2 + 1), 1280 * u : 1280 * (u + 1)].rearrange("(p j) w -> p j w", j=4),
            )
            rawu[idx] = t

        def copy_item(item, on_scalar):
            idx, seg = divmod(item, 3)
            f0, nf, c0 = SEGS[seg]
            ug = grp_alloc()
            dst = ug[:, 0 : 16 * nf].rearrange("p (h c j) -> p h c j", h=4, j=4)
            src = rawu[idx][:].rearrange("p j (h e) -> p h e j", h=4)[:, :, f0 : f0 + nf, :]
            evac(on_scalar, dst, src)
            ugrp[item] = ug
            if seg == 2 and idx + 3 < 16:
                loadu(idx + 3)

        def quant_item(item):
            idx, seg = divmod(item, 3)
            u, g2 = divmod(idx, 4)
            f0, nf, c0 = SEGS[seg]
            if seg == 0:
                cu[idx] = slot([P, 1280], U32, "cu%d" % idx, 25 + 5 * idx)
                if g2 == 0:
                    pu[u] = slot([P, 1280], U8, "pu%d" % u, 20 + 1.25 * u)
            quantize(cu[idx][:, c0 : c0 + 4 * nf], plane_rows(pu[u], g2, c0, c0 + 4 * nf), ugrp[item][:, 0 : 16 * nf])

        xload(0)
        wload0(0)
        wload0(1)
        xload(1)
        wload0(2)
        wload0(3)
        xload(2)

        def prepare(d):
            with_w = d < 8
            copy_x(d, 0)
            copy_x(d, 1)
            quant_x(d, 0)
            quant_x(d, 1)
            if with_w:
                perm_w0(2 * d)
                perm_w0(2 * d + 1)
                quant_w0(2 * d)
                quant_w0(2 * d + 1)
                if 2 * d + 5 < 16:
                    wload0(2 * d + 4)
                    wload0(2 * d + 5)

        for d in range(2):
            transposes(d)
            xload(d + 3)
            prepare(d)

        for d in range(32):
            n, gg = divmod(d, 8)
            if d + 2 < 32:
                transposes(d + 2)
                if d + 2 < FIRST_SORTED:
                    xload(d + 5)
            if 27 <= d <= 29:
                wload(2 * (d - 27))
                wload(2 * (d - 27) + 1)
            matmuls0(d)
            if FIRST_SORTED <= d + 3 < 32:
                sort_x(d + 3)
                if d + 6 < 32:
                    xload(d + 6)
            if d + 2 < 32:
                prepare(d + 2)
            if gg == 7:
                ltile = new_l(0)
                for t in range(4):
                    evac(t % 2 == 0, ltile[:, t, :], acc[t][:])
                il_queue.append((0, n, ltile))
            latent_tick()
            if 8 <= d < 15:
                table_step(d - 8)
            if d == 29:
                perm_wh(0)
                perm_wh(1)
                wload(6)
                wload(7)
            if d == 30:
                quant_wh(0)
                quant_wh(1)
                perm_wh(2)
                perm_wh(3)
                wload(8)
            if d == 31:
                quant_wh(2)

        lt = {}
        for s in range(96):
            c, hh, g = split_s(s)
            if s + 9 < 96:
                wload(s + 9)
            if s + 4 < 96:
                perm_wh(s + 4)
            if s + 3 < 96:
                quant_wh(s + 3)
            matmuls1(s)
            if g == 15 and s < 95:
                for n in range(4):
                    if hh == 0:
                        lt[n] = new_l(n)
                    for tt in range(2):
                        evac(tt == 0, lt[n][:, 2 * hh + tt, :], acc1[(n, tt)][:])
                    if hh == 1:
                        il_queue.append((c, n, lt[n]))
            latent_tick()
            if s == 70:
                loadu(0)
            if s == 81:
                loadu(1)
            if s == 82:
                loadu(2)
            if 83 <= s < 95:
                quant_item(s - 83)
            if 82 <= s < 94:
                copy_item(s - 82, (s - 82) % 3 == 2)

        evac(True, lt[0][:, 2, :], acc1[(0, 0)][:])
        evac(False, lt[0][:, 3, :], acc1[(0, 1)][:])

        def latent_now(n):
            il_queue.append((3, n, lt[n]))
            latent_tick()
            latent_tick()

        latent_now(0)
        for n in range(1, 4):
            for tt in range(2):
                evac(True, lt[n][:, 2 + tt, :], acc1[(n, tt)][:])
        latent_now(1)

        pt = {}
        GROUP_ORDER = (2, 0, 1)

        def passes(q, k, g2s):
            u, i = divmod(q, 16)
            n, ii = divmod(i, 4)
            f0, nf, c0 = SEGS[k]
            width = 4 * nf
            for g2 in g2s:
                if g2 == 0:
                    pt[(q, k)] = bank((3 * q + GROUP_ORDER.index(k) + 4) % 8)
                if g2 < 3:
                    lsc = plane_rows(latp[n], g2, P * ii, P * (ii + 1))
                else:
                    lsc = latp[(3, n)][:, P * ii : P * (ii + 1)]
                nc.tensor.matmul_mx(
                    out=pt[(q, k)][:, 0:width],
                    lhsT=lat[(g2, n)][:, P * ii : P * (ii + 1)].bitcast(FP8X4),
                    lhsT_scale=lsc,
                    rhs=cu[4 * u + g2][:, c0 : c0 + width].bitcast(FP8X4),
                    rhs_scale=plane_rows(pu[u], g2, c0, c0 + width),
                    start=(g2 == 0),
                    stop=(g2 == 3),
                )

        def finish(q):
            u, i = divmod(q, 16)
            b, a = divmod(i, 8)
            k6 = q % 6
            k2 = q % 2
            ko = slot([P, 4, 192], F32, "ko%d" % k6, 210.25 + 3 * k6)
            vo = slot([P, 512], F32, "vo%d" % k6, 115.25 + 2 * k6)
            ta = slot([P, 256], F32, "ta%d" % k2, 228.25 + k2)
            tb = slot([P, 256], F32, "tb%d" % k2, 230.25 + k2)
            nc.scalar.copy(out=ko[:, :, 0:128], in_=pt[(q, 0)][:].rearrange("p (h c) -> p h c", h=4))
            nc.scalar.copy(out=vo[:], in_=pt[(q, 1)][:])
            rope = pt[(q, 2)][:, 0:256]
            r4 = rope.rearrange("p (h s f) -> p h s f", h=4, s=2)
            tb4 = tb[:].rearrange("p (h s f) -> p h s f", h=4, s=2)
            nc.vector.tensor_tensor(
                out=ta[:].rearrange("p (e f) -> p e f", f=32),
                in0=rope.rearrange("p (e f) -> p e f", f=32),
                in1=tab[:, 0, a, :].unsqueeze(1).to_broadcast([P, 8, 32]),
                op=ALU.mult,
            )
            for half in range(2):
                nc.vector.tensor_tensor(
                    out=tb4[:, :, half, :],
                    in0=r4[:, :, 1 - half, :],
                    in1=tab[:, 1 + half, a, :].unsqueeze(1).to_broadcast([P, 4, 32]),
                    op=ALU.mult,
                )
            nc.vector.tensor_tensor(
                out=ko[:, :, 128:192],
                in0=ta[:].rearrange("p (h e) -> p h e", h=4),
                in1=tb[:].rearrange("p (h e) -> p h e", h=4),
                op=ALU.add,
            )
            rows = slice(P * a, P * (a + 1))
            heads = slice(4 * u, 4 * (u + 1))
            nc.sync.dma_start(out=out_v[b, rows, heads, :], in_=vo[:].rearrange("p (h c) -> p h c", h=4))
            nc.sync.dma_start(out=out_k[b, rows, heads, :], in_=ko[:])

        items = {"copied": 12, "quantized": 12}

        def produce(q):
            if items["quantized"] < items["copied"]:
                quant_item(items["quantized"])
                items["quantized"] += 1
            if (q < 12 or q % 4 != 3) and items["copied"] < 48:
                copy_item(items["copied"], items["copied"] % 3 != 0)
                items["copied"] += 1

        for q in range(2):
            for k in GROUP_ORDER:
                passes(q, k, (0, 1, 2))
        for q in range(2):
            for k in GROUP_ORDER:
                passes(q, k, (3,))
            finish(q)
            latent_now(2 + q)
            produce(q)
        for q in range(2, 64):
            for k in GROUP_ORDER:
                passes(q, k, (0, 1, 2, 3))
            finish(q)
            produce(q)
